import numpy as np
import ml_dtypes


def mxq(x, axis, fmt="e4m3"):
    dtype, down = {"e4m3": (ml_dtypes.float8_e4m3fn, 7), "e5m2": (ml_dtypes.float8_e5m2, 14)}[fmt]
    v = np.moveaxis(np.asarray(x, np.float32).astype(ml_dtypes.bfloat16).astype(np.float64), axis, -1)
    blocks = v.reshape(v.shape[:-1] + (-1, 32))
    amax = np.abs(blocks).max(-1, keepdims=True)
    byte = np.maximum(np.where(amax > 0, np.frexp(amax)[1] - 1 + 127, 0) - down, 1)
    scale = np.exp2(byte - 127.0)
    codes = (blocks / scale).astype(np.float32).astype(dtype).astype(np.float64)
    return np.moveaxis((codes * scale).reshape(v.shape), -1, axis)


WIDE = False


def mx_kscale(k):
    if not WIDE:
        return np.ones(k)
    levels = np.array([10, -10, 5, -5, 0])
    a = np.random.permutation(np.resize(levels, k // 512 * 4)).reshape(k // 512, 4)
    idx = np.arange(k)
    return np.exp2(a[idx // 512, idx % 128 // 32])


BF16 = ml_dtypes.bfloat16


def bf(x):
    return np.asarray(x, np.float32).astype(BF16)


def f64(x):
    return np.asarray(x).astype(np.float64)


E2M1 = np.array([0.0, 0.5, 1.0, 1.5, 2.0, 3.0, 4.0, 6.0, -0.0, -0.5, -1.0, -1.5, -2.0, -3.0, -4.0, -6.0])


def pack_weight(w, fmt):
    k, n = w.shape
    w = f64(bf(w)).reshape(k // 32, 32, n)
    amax = np.abs(w).max(1)
    if fmt == "e4m3":
        byte = np.frexp(amax)[1] - 1 + 127 - 7
    else:
        mant, ex = np.frexp(amax / 6.0)
        byte = np.where(mant > 0.5, ex, ex - 1) + 127
    byte = np.clip(np.where(amax > 0, byte, 1), 1, 254)
    scaled = (w * np.exp2(127.0 - byte)[:, None, :]).reshape(k, n).astype(np.float32)
    by_word = np.ascontiguousarray(scaled.reshape(k // 512, 128, 4, n).transpose(0, 1, 3, 2))
    if fmt == "e4m3":
        words = by_word.astype(ml_dtypes.float8_e4m3fn).view(np.uint8)
    else:
        c = by_word.astype(ml_dtypes.float4_e2m1fn).view(np.uint8) & 0xF
        words = c[..., 0::2] | (c[..., 1::2] << 4)
    return np.ascontiguousarray(words), np.ascontiguousarray(byte.astype(np.uint8).reshape(k // 512, 16, n))


def unpack_weight(words, scales, fmt):
    g, p, n, _ = words.shape
    if fmt == "e4m3":
        vals = np.ascontiguousarray(words).view(ml_dtypes.float8_e4m3fn).astype(np.float64)
    else:
        nib = np.empty((g, p, n, 4), np.uint8)
        nib[..., 0::2] = words & 0xF
        nib[..., 1::2] = words >> 4
        vals = E2M1[nib]
    vals = vals * np.repeat(np.exp2(scales.astype(np.float64) - 127.0), 8, axis=1)[..., None]
    return vals.transpose(0, 1, 3, 2).reshape(g * 512, n)


B, T, C, H, G, D = 2, 64, 8192, 8, 2, 128
EPS = 1e-6
FMT = "e4m3"


def rmsnorm(v, w):
    return v / np.sqrt(np.mean(v * v, axis=-1, keepdims=True) + EPS) * w


def apply_rotary(v, cos, sin):
    v1, v2 = np.split(v, 2, axis=-1)
    return np.concatenate([v1 * cos - v2 * sin, v1 * sin + v2 * cos], axis=-1)


def setup_inputs():
    s = mx_kscale(C)
    ang = np.arange(T)[:, None] / 10000.0 ** (np.arange(0, D, 2) / D)[None, :]
    a = 4.0 * np.sqrt(EPS / C)
    x = bf(np.random.standard_normal((B, T, C)) * s)
    cos = bf(np.cos(ang)[None, None, :, :])
    sin = bf(np.sin(ang)[None, None, :, :])
    wq = np.random.standard_normal((G * H * D, C)) * a / s[None, :]
    wk = np.random.standard_normal((H * D, C)) * a / s[None, :]
    wv = np.random.standard_normal((H * D, C)) / np.sqrt(C) / s[None, :]
    q_norm_w = bf(1.0 + 0.1 * np.random.standard_normal(D))
    k_norm_w = bf(1.0 + 0.1 * np.random.standard_normal(D))
    wq_words, wq_scales = pack_weight(np.ascontiguousarray(wq.T), FMT)
    wk_words, wk_scales = pack_weight(np.ascontiguousarray(wk.T), FMT)
    wv_words, wv_scales = pack_weight(np.ascontiguousarray(wv.T), FMT)
    return {"x": x,
            "cos": cos,
            "sin": sin,
            "wq_words": wq_words, "wq_scales": wq_scales,
            "wk_words": wk_words, "wk_scales": wk_scales,
            "wv_words": wv_words, "wv_scales": wv_scales,
            "q_norm_w": q_norm_w,
            "k_norm_w": k_norm_w}


def reference(x, cos, sin, wq_words, wq_scales, wk_words, wk_scales, wv_words, wv_scales, q_norm_w, k_norm_w):
    xq = mxq(f64(x), 2, "e4m3")
    q = (xq @ unpack_weight(wq_words, wq_scales, FMT)).reshape(B, T, G * H, D).transpose(0, 2, 1, 3)
    k = (xq @ unpack_weight(wk_words, wk_scales, FMT)).reshape(B, T, H, D).transpose(0, 2, 1, 3)
    v = (xq @ unpack_weight(wv_words, wv_scales, FMT)).reshape(B, T, H, D).transpose(0, 2, 1, 3)
    q = rmsnorm(q, f64(q_norm_w))
    k = rmsnorm(k, f64(k_norm_w))
    c, sn = f64(cos)[:, :, :T, :], f64(sin)[:, :, :T, :]
    q = apply_rotary(q, c, sn)
    k = apply_rotary(k, c, sn)
    return q, k, v

@@ -1,0 +1,242 @@
+from contextlib import ExitStack
+
+import concourse.mybir as mybir
+from concourse.masks import make_identity
+
+F32 = mybir.dt.float32
+BF16 = mybir.dt.bfloat16
+U8 = mybir.dt.uint8
+I32 = mybir.dt.int32
+U32 = mybir.dt.uint32
+FP8X4 = mybir.dt.float8_e4m3fn_x4
+MULT = mybir.AluOpType.mult
+ADD = mybir.AluOpType.add
+
+P = 128
+PACK = 4
+K_PASS = P * PACK
+BATCH = 2
+FEATURES = 8192
+GROUPS = FEATURES // K_PASS
+HEAD = 128
+HALF = HEAD // 2
+Q_COLS = 2048
+K_COLS = 1024
+V_COLS = 1024
+BANK = 512
+HEADS_PER_BANK = BANK // HEAD
+EPS = 1e-6
+
+SHARED = 4
+LIVE_ROWS = 4
+QUADRANTS = 4
+
+X_PIECES = 4
+GROUPS_PER_PIECE = GROUPS // X_PIECES
+WORDS_PER_GROUP = K_PASS // 2
+
+LOAD_WORDS = 2048
+W_BUFS = 12
+
+FLOPS = 2 * P * FEATURES * (Q_COLS + K_COLS + V_COLS)
+
+
+def tile_qwen3attention_pa_k_kernel(
+    tc, x, cos, sin, wq_words, wq_scales, wk_words, wk_scales, wv_words, wv_scales,
+    q_norm_w, k_norm_w, out_0, out_1, out_2,
+):
+    nc = tc.nc
+    with ExitStack() as ctx:
+        ctx.enter_context(tc.manual_schedule())
+        keep = ctx.enter_context(tc.tile_pool(name="keep", bufs=1))
+        stream = ctx.enter_context(tc.tile_pool(name="stream", bufs=W_BUFS))
+        work = ctx.enter_context(tc.tile_pool(name="work", bufs=1))
+        psum = ctx.enter_context(tc.psum_pool(name="psum", bufs=8))
+
+        x_sb = keep.tile([P, FEATURES], BF16)
+        piece_cols = FEATURES // X_PIECES
+        for piece in range(X_PIECES):
+            cols = slice(piece * piece_cols, (piece + 1) * piece_cols)
+            for b in range(BATCH):
+                nc.sync.dma_start(out=x_sb[b:P:BATCH, cols], in_=x[b][:, cols])
+
+        def load_scale_planes(scales, n_cols, label):
+            planes = keep.tile([P, (GROUPS // SHARED) * n_cols], U8, align_bytes=64, name="planes_" + label)
+            nc.vector.memset(planes[:].bitcast(I32), 0)
+            for c in range(GROUPS // SHARED):
+                for quadrant in range(QUADRANTS):
+                    first_row = 32 * quadrant
+                    nc.sync.dma_start(
+                        out=planes[first_row : first_row + SHARED * LIVE_ROWS, c * n_cols : (c + 1) * n_cols].bitcast(I32),
+                        in_=scales[
+                            SHARED * c : SHARED * (c + 1), LIVE_ROWS * quadrant : LIVE_ROWS * (quadrant + 1), :
+                        ].bitcast(I32),
+                    )
+            return planes
+
+        q_planes = load_scale_planes(wq_scales, Q_COLS, "q")
+        k_planes = load_scale_planes(wk_scales, K_COLS, "k")
+        v_planes = load_scale_planes(wv_scales, V_COLS, "v")
+
+        identity = keep.tile([P, P], F32)
+        make_identity(nc, identity[:])
+        cos_sb = keep.tile([P, HALF], BF16)
+        sin_sb = keep.tile([P, HALF], BF16)
+        gain_rows = keep.tile([P, 2 * HEAD], BF16)
+        ones = keep.tile([P, P], BF16)
+        nc.vector.memset(gain_rows[:], 0.0)
+        nc.vector.memset(ones[:], 1.0)
+        nc.gpsimd.dma_start(out=gain_rows[0:1, 0:HEAD], in_=q_norm_w.unsqueeze(0))
+        nc.gpsimd.dma_start(out=gain_rows[0:1, HEAD : 2 * HEAD], in_=k_norm_w.unsqueeze(0))
+        for b in range(BATCH):
+            nc.gpsimd.dma_start(out=cos_sb[b:P:BATCH, :], in_=cos[0, 0])
+            nc.gpsimd.dma_start(out=sin_sb[b:P:BATCH, :], in_=sin[0, 0])
+
+        x_words = x_sb[:].bitcast(F32)
+        x_grouped = keep.tile([P, GROUPS * P * PACK], BF16, align_bytes=64)
+        grouped_words = x_grouped[:].bitcast(F32)
+        x_codes = keep.tile([P, GROUPS * P], U32, align_bytes=64)
+        x_plane = keep.tile([P, GROUPS * P], U8, align_bytes=64)
+        groups_per_bank = BANK // (2 * P)
+        banks_per_piece = GROUPS_PER_PIECE // groups_per_bank
+        for piece in range(X_PIECES):
+            for half_piece in range(banks_per_piece):
+                bank = piece * banks_per_piece + half_piece
+                flipped = psum.tile([P, BANK], F32, tag="bank")
+                for i in range(groups_per_bank):
+                    g = bank * groups_per_bank + i
+                    for u in range(2):
+                        nc.tensor.transpose(
+                            out=flipped[:, (2 * i + u) * P : (2 * i + u + 1) * P],
+                            in_=x_words[:, WORDS_PER_GROUP * g + u : WORDS_PER_GROUP * (g + 1) : 2],
+                            identity=identity[:],
+                        )
+                copy_out = nc.vector.tensor_copy if bank % 2 == 0 else nc.scalar.copy
+                copy_out(
+                    out=grouped_words[:, bank * BANK : (bank + 1) * BANK].rearrange(
+                        "p (g r u) -> p g r u", g=groups_per_bank, u=2
+                    ),
+                    in_=flipped[:].rearrange("p (g u r) -> p g r u", g=groups_per_bank, u=2),
+                )
+            tokens = slice(piece * GROUPS_PER_PIECE * P, (piece + 1) * GROUPS_PER_PIECE * P)
+            nc.vector.quantize_mx(
+                out=x_codes[:, tokens].bitcast(FP8X4),
+                scales=x_plane[:, tokens],
+                in_=x_grouped[:, piece * GROUPS_PER_PIECE * K_PASS : (piece + 1) * GROUPS_PER_PIECE * K_PASS],
+            )
+
+        gains = psum.tile([P, BANK], F32, tag="bank")
+        nc.tensor.matmul(out=gains[:, 0 : 2 * HEAD], lhsT=ones[:], rhs=gain_rows[:], start=True, stop=True)
+        gains_by_half = gains[:, 0 : 2 * HEAD].rearrange("p (w h d) -> p w h d", w=2, h=2)
+        neg_sin = keep.tile([P, HALF], F32)
+        nc.vector.tensor_scalar_mul(out=neg_sin[:], in0=sin_sb[:], scalar1=-1.0)
+        straight = keep.tile([P, 2, 2, HALF], F32)
+        crossed = keep.tile([P, 2, 2, HALF], F32)
+        nc.vector.tensor_tensor(
+            out=straight[:].rearrange("p w h d -> p (w h) d"),
+            in0=gains[:, 0 : 2 * HEAD].rearrange("p (a d) -> p a d", d=HALF),
+            in1=cos_sb[:].unsqueeze(1).to_broadcast([P, 4, HALF]),
+            op=MULT,
+        )
+        nc.vector.tensor_tensor(
+            out=crossed[:, :, 0, :], in0=gains_by_half[:, :, 1, :],
+            in1=neg_sin[:].unsqueeze(1).to_broadcast([P, 2, HALF]), op=MULT,
+        )
+        nc.vector.tensor_tensor(
+            out=crossed[:, :, 1, :], in0=gains_by_half[:, :, 0, :],
+            in1=sin_sb[:].unsqueeze(1).to_broadcast([P, 2, HALF]), op=MULT,
+        )
+
+        def project(words, planes, n_cols, label):
+            banks = [
+                psum.tile([P, BANK], F32, tag="bank", name="acc_%s_%d" % (label, j)) for j in range(n_cols // BANK)
+            ]
+            groups_per_load = LOAD_WORDS // n_cols
+            for first_g in range(0, GROUPS, groups_per_load):
+                w_sb = stream.tile([P, LOAD_WORDS], I32, align_bytes=64, tag="w")
+                nc.sync.dma_start(
+                    out=w_sb[:].rearrange("p (g n) -> p g n", g=groups_per_load),
+                    in_=words[first_g : first_g + groups_per_load].rearrange("g p n j -> p g (n j)").bitcast(I32),
+                )
+                for i in range(groups_per_load):
+                    g = first_g + i
+                    first = LIVE_ROWS * (g % SHARED)
+                    for j, acc in enumerate(banks):
+                        nc.tensor.matmul_mx(
+                            out=acc[:],
+                            lhsT=x_codes[:, g * P : (g + 1) * P].bitcast(FP8X4),
+                            lhsT_scale=x_plane[:, g * P : (g + 1) * P],
+                            rhs=w_sb[:, i * n_cols + j * BANK : i * n_cols + (j + 1) * BANK].bitcast(FP8X4),
+                            rhs_scale=planes[
+                                first:P, (g // SHARED) * n_cols + j * BANK : (g // SHARED) * n_cols + (j + 1) * BANK
+                            ],
+                            start=(g == 0),
+                            stop=(g == GROUPS - 1),
+                        )
+            return banks
+
+        def store(result, out, queue):
+            for b in range(BATCH):
+                queue.dma_start(
+                    out=out[b].rearrange("h t d -> t h d"),
+                    in_=result[b:P:BATCH, :].rearrange("p (h d) -> p h d", d=HEAD),
+                )
+
+        def norm_and_rotate(banks, weight, out):
+            heads = len(banks) * HEADS_PER_BANK
+            squares = work.tile([P, heads * HEAD], F32, tag="squares")
+            straight_part = work.tile([P, heads * HEAD], F32, tag="straight_part")
+            crossed_part = work.tile([P, heads * HEAD], F32, tag="crossed_part")
+            result = work.tile([P, heads * HEAD], F32, tag="result", bufs=2)
+            sum_sq = work.tile([P, heads], F32, tag="sum_sq")
+            mean_sq = work.tile([P, heads], F32, tag="mean_sq")
+            rms = work.tile([P, heads], F32, tag="rms")
+            inv_rms = work.tile([P, heads], F32, tag="inv_rms")
+            for j, acc in enumerate(banks):
+                cols = slice(j * BANK, (j + 1) * BANK)
+                nc.scalar.square(out=squares[:, cols], in_=acc[:])
+                nc.vector.tensor_reduce(
+                    out=sum_sq[:, j * HEADS_PER_BANK : (j + 1) * HEADS_PER_BANK],
+                    in_=squares[:, cols].rearrange("p (h d) -> p h d", d=HEAD),
+                    axis=mybir.AxisListType.X,
+                    op=ADD,
+                )
+                nc.vector.tensor_tensor(
+                    out=straight_part[:, cols].rearrange("p (h d) -> p h d", d=HEAD),
+                    in0=acc[:].rearrange("p (h d) -> p h d", d=HEAD),
+                    in1=straight[:, weight].rearrange("p h d -> p (h d)").unsqueeze(1).to_broadcast(
+                        [P, HEADS_PER_BANK, HEAD]
+                    ),
+                    op=MULT,
+                )
+                acc_halves = acc[:].rearrange("p (h s d) -> p h s d", s=2, d=HALF)
+                crossed_halves = crossed_part[:, cols].rearrange("p (h s d) -> p h s d", s=2, d=HALF)
+                for s in range(2):
+                    nc.vector.tensor_tensor(
+                        out=crossed_halves[:, :, s, :],
+                        in0=acc_halves[:, :, 1 - s, :],
+                        in1=crossed[:, weight, s, :].unsqueeze(1).to_broadcast([P, HEADS_PER_BANK, HALF]),
+                        op=MULT,
+                    )
+            nc.vector.tensor_scalar(
+                out=mean_sq[:], in0=sum_sq[:], scalar1=1.0 / HEAD, scalar2=EPS, op0=MULT, op1=ADD
+            )
+            nc.scalar.sqrt(out=rms[:], in_=mean_sq[:])
+            nc.vector.reciprocal(out=inv_rms[:], in_=rms[:])
+            nc.vector.tensor_tensor(out=straight_part[:], in0=straight_part[:], in1=crossed_part[:], op=ADD)
+            nc.vector.tensor_tensor(
+                out=result[:].rearrange("p (h d) -> p h d", d=HEAD),
+                in0=straight_part[:].rearrange("p (h d) -> p h d", d=HEAD),
+                in1=inv_rms[:].unsqueeze(2).to_broadcast([P, heads, HEAD]),
+                op=MULT,
+            )
+            store(result, out, nc.scalar)
+
+        norm_and_rotate(project(wq_words, q_planes, Q_COLS, "q"), 0, out_0)
+        norm_and_rotate(project(wk_words, k_planes, K_COLS, "k"), 1, out_1)
+
+        v_banks = project(wv_words, v_planes, V_COLS, "v")
+        v_result = work.tile([P, V_COLS], F32, tag="result", bufs=2)
+        nc.vector.tensor_copy(out=v_result[:, 0:BANK], in_=v_banks[0][:])
+        nc.scalar.copy(out=v_result[:, BANK : 2 * BANK], in_=v_banks[1][:])
+        store(v_result, out_2, nc.sync)

@@ -60,24 +60,6 @@ def tile_qwen3attention_pa_k_kernel(
             for b in range(BATCH):
                 nc.sync.dma_start(out=x_sb[b:P:BATCH, cols], in_=x[b][:, cols])
 
-        def load_scale_planes(scales, n_cols, label):
-            planes = keep.tile([P, (GROUPS // SHARED) * n_cols], U8, align_bytes=64, name="planes_" + label)
-            nc.vector.memset(planes[:].bitcast(I32), 0)
-            for c in range(GROUPS // SHARED):
-                for quadrant in range(QUADRANTS):
-                    first_row = 32 * quadrant
-                    nc.sync.dma_start(
-                        out=planes[first_row : first_row + SHARED * LIVE_ROWS, c * n_cols : (c + 1) * n_cols].bitcast(I32),
-                        in_=scales[
-                            SHARED * c : SHARED * (c + 1), LIVE_ROWS * quadrant : LIVE_ROWS * (quadrant + 1), :
-                        ].bitcast(I32),
-                    )
-            return planes
-
-        q_planes = load_scale_planes(wq_scales, Q_COLS, "q")
-        k_planes = load_scale_planes(wk_scales, K_COLS, "k")
-        v_planes = load_scale_planes(wv_scales, V_COLS, "v")
-
         identity = keep.tile([P, P], F32)
         make_identity(nc, identity[:])
         cos_sb = keep.tile([P, HALF], BF16)
@@ -91,6 +73,24 @@ def tile_qwen3attention_pa_k_kernel(
         for b in range(BATCH):
             nc.gpsimd.dma_start(out=cos_sb[b:P:BATCH, :], in_=cos[0, 0])
             nc.gpsimd.dma_start(out=sin_sb[b:P:BATCH, :], in_=sin[0, 0])
+
+        def load_scale_planes(scales, n_cols, label):
+            planes = keep.tile([P, (GROUPS // SHARED) * n_cols], U8, align_bytes=64, name="planes_" + label)
+            nc.vector.memset(planes[:].bitcast(I32), 0)
+            for c in range(GROUPS // SHARED):
+                for quadrant in range(QUADRANTS):
+                    first_row = 32 * quadrant
+                    nc.gpsimd.dma_start(
+                        out=planes[first_row : first_row + SHARED * LIVE_ROWS, c * n_cols : (c + 1) * n_cols].bitcast(F32),
+                        in_=scales[
+                            SHARED * c : SHARED * (c + 1), LIVE_ROWS * quadrant : LIVE_ROWS * (quadrant + 1), :
+                        ].bitcast(F32),
+                    )
+            return planes
+
+        q_planes = load_scale_planes(wq_scales, Q_COLS, "q")
+        k_planes = load_scale_planes(wk_scales, K_COLS, "k")
+        v_planes = load_scale_planes(wv_scales, V_COLS, "v")
 
         x_words = x_sb[:].bitcast(F32)
         x_grouped = keep.tile([P, GROUPS * P * PACK], BF16, align_bytes=64)

@@ -37,6 +37,7 @@ WORDS_PER_GROUP = K_PASS // 2
 
 LOAD_WORDS = 2048
 W_BUFS = 12
+RESULTS = 3
 
 FLOPS = 2 * P * FEATURES * (Q_COLS + K_COLS + V_COLS)
 
@@ -175,19 +176,19 @@ def tile_qwen3attention_pa_k_kernel(
                         )
             return banks
 
-        def store(result, out, queue):
+        def store(result, out):
             for b in range(BATCH):
-                queue.dma_start(
+                nc.sync.dma_start(
                     out=out[b].rearrange("h t d -> t h d"),
                     in_=result[b:P:BATCH, :].rearrange("p (h d) -> p h d", d=HEAD),
                 )
 
-        def norm_and_rotate(banks, weight, out):
+        def norm_and_rotate(banks, weight):
             heads = len(banks) * HEADS_PER_BANK
             squares = work.tile([P, heads * HEAD], F32, tag="squares")
             straight_part = work.tile([P, heads * HEAD], F32, tag="straight_part")
             crossed_part = work.tile([P, heads * HEAD], F32, tag="crossed_part")
-            result = work.tile([P, heads * HEAD], F32, tag="result", bufs=2)
+            result = work.tile([P, heads * HEAD], F32, tag="result", bufs=RESULTS)
             sum_sq = work.tile([P, heads], F32, tag="sum_sq")
             mean_sq = work.tile([P, heads], F32, tag="mean_sq")
             rms = work.tile([P, heads], F32, tag="rms")
@@ -230,13 +231,14 @@ def tile_qwen3attention_pa_k_kernel(
                 in1=inv_rms[:].unsqueeze(2).to_broadcast([P, heads, HEAD]),
                 op=MULT,
             )
-            store(result, out, nc.scalar)
+            return result
 
-        norm_and_rotate(project(wq_words, q_planes, Q_COLS, "q"), 0, out_0)
-        norm_and_rotate(project(wk_words, k_planes, K_COLS, "k"), 1, out_1)
-
+        q_result = norm_and_rotate(project(wq_words, q_planes, Q_COLS, "q"), 0)
+        k_result = norm_and_rotate(project(wk_words, k_planes, K_COLS, "k"), 1)
         v_banks = project(wv_words, v_planes, V_COLS, "v")
-        v_result = work.tile([P, V_COLS], F32, tag="result", bufs=2)
+        store(q_result, out_0)
+        store(k_result, out_1)
+        v_result = work.tile([P, V_COLS], F32, tag="result", bufs=RESULTS)
         nc.vector.tensor_copy(out=v_result[:, 0:BANK], in_=v_banks[0][:])
         nc.scalar.copy(out=v_result[:, BANK : 2 * BANK], in_=v_banks[1][:])
-        store(v_result, out_2, nc.sync)
+        store(v_result, out_2)

@@ -58,8 +58,35 @@ def tile_qwen3attention_pa_k_kernel(
         piece_cols = FEATURES // X_PIECES
         for piece in range(X_PIECES):
             cols = slice(piece * piece_cols, (piece + 1) * piece_cols)
-            for b in range(BATCH):
-                nc.sync.dma_start(out=x_sb[b:P:BATCH, cols], in_=x[b][:, cols])
+            nc.sync.dma_start(out=x_sb[0:P:BATCH, cols], in_=x[0][:, cols])
+            nc.scalar.dma_start(out=x_sb[1:P:BATCH, cols], in_=x[1][:, cols])
+
+        weights = ((wq_words, Q_COLS), (wk_words, K_COLS), (wv_words, V_COLS))
+        plan = []
+        for w_index in range(len(weights)):
+            for first_g in range(0, GROUPS, LOAD_WORDS // weights[w_index][1]):
+                plan.append((w_index, first_g))
+        loaded = []
+
+        def issue(n):
+            words, n_cols = weights[plan[n][0]]
+            first_g = plan[n][1]
+            groups_per_load = LOAD_WORDS // n_cols
+            w_sb = stream.tile([P, LOAD_WORDS], I32, align_bytes=64, tag="w", name="w_%d" % n)
+            source = words[first_g : first_g + groups_per_load].rearrange("g p n j -> p g (n j)")
+            if n % 2 == 1 and n != len(plan) - 1:
+                nc.scalar.dma_start(
+                    out=w_sb[:].bitcast(F32).rearrange("p (g n) -> p g n", g=groups_per_load),
+                    in_=source.bitcast(F32),
+                )
+            else:
+                nc.sync.dma_start(
+                    out=w_sb[:].rearrange("p (g n) -> p g n", g=groups_per_load), in_=source.bitcast(I32)
+                )
+            loaded.append(w_sb)
+
+        for n in range(W_BUFS):
+            issue(n)
 
         identity = keep.tile([P, P], F32)
         make_identity(nc, identity[:])
@@ -148,33 +175,32 @@ def tile_qwen3attention_pa_k_kernel(
             in1=sin_sb[:].unsqueeze(1).to_broadcast([P, 2, HALF]), op=MULT,
         )
 
-        def project(words, planes, n_cols, label):
-            banks = [
+        def open_banks(n_cols, label):
+            return [
                 psum.tile([P, BANK], F32, tag="bank", name="acc_%s_%d" % (label, j)) for j in range(n_cols // BANK)
             ]
-            groups_per_load = LOAD_WORDS // n_cols
-            for first_g in range(0, GROUPS, groups_per_load):
-                w_sb = stream.tile([P, LOAD_WORDS], I32, align_bytes=64, tag="w")
-                nc.sync.dma_start(
-                    out=w_sb[:].rearrange("p (g n) -> p g n", g=groups_per_load),
-                    in_=words[first_g : first_g + groups_per_load].rearrange("g p n j -> p g (n j)").bitcast(I32),
-                )
-                for i in range(groups_per_load):
-                    g = first_g + i
-                    first = LIVE_ROWS * (g % SHARED)
-                    for j, acc in enumerate(banks):
-                        nc.tensor.matmul_mx(
-                            out=acc[:],
-                            lhsT=x_codes[:, g * P : (g + 1) * P].bitcast(FP8X4),
-                            lhsT_scale=x_plane[:, g * P : (g + 1) * P],
-                            rhs=w_sb[:, i * n_cols + j * BANK : i * n_cols + (j + 1) * BANK].bitcast(FP8X4),
-                            rhs_scale=planes[
-                                first:P, (g // SHARED) * n_cols + j * BANK : (g // SHARED) * n_cols + (j + 1) * BANK
-                            ],
-                            start=(g == 0),
-                            stop=(g == GROUPS - 1),
-                        )
-            return banks
+
+        def multiply(n, planes, banks):
+            n_cols = weights[plan[n][0]][1]
+            first_g = plan[n][1]
+            w_sb = loaded[n]
+            for i in range(LOAD_WORDS // n_cols):
+                g = first_g + i
+                first = LIVE_ROWS * (g % SHARED)
+                for j, acc in enumerate(banks):
+                    nc.tensor.matmul_mx(
+                        out=acc[:],
+                        lhsT=x_codes[:, g * P : (g + 1) * P].bitcast(FP8X4),
+                        lhsT_scale=x_plane[:, g * P : (g + 1) * P],
+                        rhs=w_sb[:, i * n_cols + j * BANK : i * n_cols + (j + 1) * BANK].bitcast(FP8X4),
+                        rhs_scale=planes[
+                            first:P, (g // SHARED) * n_cols + j * BANK : (g // SHARED) * n_cols + (j + 1) * BANK
+                        ],
+                        start=(g == 0),
+                        stop=(g == GROUPS - 1),
+                    )
+            if n + W_BUFS < len(plan):
+                issue(n + W_BUFS)
 
         def store(result, out):
             for b in range(BATCH):
@@ -219,23 +245,41 @@ def tile_qwen3attention_pa_k_kernel(
                         in1=crossed[:, weight, s, :].unsqueeze(1).to_broadcast([P, HEADS_PER_BANK, HALF]),
                         op=MULT,
                     )
-            nc.vector.tensor_scalar(
-                out=mean_sq[:], in0=sum_sq[:], scalar1=1.0 / HEAD, scalar2=EPS, op0=MULT, op1=ADD
-            )
-            nc.scalar.sqrt(out=rms[:], in_=mean_sq[:])
-            nc.vector.reciprocal(out=inv_rms[:], in_=rms[:])
-            nc.vector.tensor_tensor(out=straight_part[:], in0=straight_part[:], in1=crossed_part[:], op=ADD)
-            nc.vector.tensor_tensor(
-                out=result[:].rearrange("p (h d) -> p h d", d=HEAD),
-                in0=straight_part[:].rearrange("p (h d) -> p h d", d=HEAD),
-                in1=inv_rms[:].unsqueeze(2).to_broadcast([P, heads, HEAD]),
-                op=MULT,
-            )
-            return result
 
-        q_result = norm_and_rotate(project(wq_words, q_planes, Q_COLS, "q"), 0)
-        k_result = norm_and_rotate(project(wk_words, k_planes, K_COLS, "k"), 1)
-        v_banks = project(wv_words, v_planes, V_COLS, "v")
+            def finish():
+                nc.vector.tensor_scalar(
+                    out=mean_sq[:], in0=sum_sq[:], scalar1=1.0 / HEAD, scalar2=EPS, op0=MULT, op1=ADD
+                )
+                nc.scalar.sqrt(out=rms[:], in_=mean_sq[:])
+                nc.vector.reciprocal(out=inv_rms[:], in_=rms[:])
+                nc.vector.tensor_tensor(out=straight_part[:], in0=straight_part[:], in1=crossed_part[:], op=ADD)
+                nc.vector.tensor_tensor(
+                    out=result[:].rearrange("p (h d) -> p h d", d=HEAD),
+                    in0=straight_part[:].rearrange("p (h d) -> p h d", d=HEAD),
+                    in1=inv_rms[:].unsqueeze(2).to_broadcast([P, heads, HEAD]),
+                    op=MULT,
+                )
+                return result
+
+            return finish
+
+        q_loads = GROUPS * Q_COLS // LOAD_WORDS
+        k_loads = GROUPS * K_COLS // LOAD_WORDS
+        all_issued = len(plan) - W_BUFS
+        q_banks = open_banks(Q_COLS, "q")
+        for n in range(q_loads):
+            multiply(n, q_planes, q_banks)
+        finish_q = norm_and_rotate(q_banks, 0)
+        k_banks = open_banks(K_COLS, "k")
+        for n in range(q_loads, all_issued):
+            multiply(n, k_planes, k_banks)
+        q_result = finish_q()
+        for n in range(all_issued, q_loads + k_loads):
+            multiply(n, k_planes, k_banks)
+        k_result = norm_and_rotate(k_banks, 1)()
+        v_banks = open_banks(V_COLS, "v")
+        for n in range(q_loads + k_loads, len(plan)):
+            multiply(n, v_planes, v_banks)
         store(q_result, out_0)
         store(k_result, out_1)
         v_result = work.tile([P, V_COLS], F32, tag="result", bufs=RESULTS)

@@ -54,12 +54,22 @@ def tile_qwen3attention_pa_k_kernel(
         work = ctx.enter_context(tc.tile_pool(name="work", bufs=1))
         psum = ctx.enter_context(tc.psum_pool(name="psum", bufs=8))
 
+        identity = keep.tile([P, P], F32)
+        make_identity(nc, identity[:])
+        cos_sb = keep.tile([P, HALF], BF16)
+        sin_sb = keep.tile([P, HALF], BF16)
+        gain_rows = keep.tile([P, 2 * HEAD], BF16)
+        ones = keep.tile([P, P], BF16)
+        nc.vector.memset(gain_rows[:], 0.0)
+        nc.vector.memset(ones[:], 1.0)
+        for b in range(BATCH):
+            nc.scalar.dma_start(out=cos_sb[b:P:BATCH, :], in_=cos[0, 0])
+            nc.scalar.dma_start(out=sin_sb[b:P:BATCH, :], in_=sin[0, 0])
         x_sb = keep.tile([P, FEATURES], BF16)
-        piece_cols = FEATURES // X_PIECES
-        for piece in range(X_PIECES):
-            cols = slice(piece * piece_cols, (piece + 1) * piece_cols)
-            nc.sync.dma_start(out=x_sb[0:P:BATCH, cols], in_=x[0][:, cols])
-            nc.scalar.dma_start(out=x_sb[1:P:BATCH, cols], in_=x[1][:, cols])
+        nc.sync.dma_start(out=x_sb[0:P:BATCH, :], in_=x[0])
+        nc.scalar.dma_start(out=x_sb[1:P:BATCH, :], in_=x[1])
+        nc.scalar.dma_start(out=gain_rows[0:1, 0:HEAD], in_=q_norm_w.unsqueeze(0))
+        nc.scalar.dma_start(out=gain_rows[0:1, HEAD : 2 * HEAD], in_=k_norm_w.unsqueeze(0))
 
         weights = ((wq_words, Q_COLS), (wk_words, K_COLS), (wv_words, V_COLS))
         plan = []
@@ -87,20 +97,6 @@ def tile_qwen3attention_pa_k_kernel(
 
         for n in range(W_BUFS):
             issue(n)
-
-        identity = keep.tile([P, P], F32)
-        make_identity(nc, identity[:])
-        cos_sb = keep.tile([P, HALF], BF16)
-        sin_sb = keep.tile([P, HALF], BF16)
-        gain_rows = keep.tile([P, 2 * HEAD], BF16)
-        ones = keep.tile([P, P], BF16)
-        nc.vector.memset(gain_rows[:], 0.0)
-        nc.vector.memset(ones[:], 1.0)
-        nc.gpsimd.dma_start(out=gain_rows[0:1, 0:HEAD], in_=q_norm_w.unsqueeze(0))
-        nc.gpsimd.dma_start(out=gain_rows[0:1, HEAD : 2 * HEAD], in_=k_norm_w.unsqueeze(0))
-        for b in range(BATCH):
-            nc.gpsimd.dma_start(out=cos_sb[b:P:BATCH, :], in_=cos[0, 0])
-            nc.gpsimd.dma_start(out=sin_sb[b:P:BATCH, :], in_=sin[0, 0])
 
         def load_scale_planes(scales, n_cols, label):
             planes = keep.tile([P, (GROUPS // SHARED) * n_cols], U8, align_bytes=64, name="planes_" + label)

@@ -65,7 +65,7 @@ def tile_qwen3attention_pa_k_kernel(
         for b in range(BATCH):
             nc.scalar.dma_start(out=cos_sb[b:P:BATCH, :], in_=cos[0, 0])
             nc.scalar.dma_start(out=sin_sb[b:P:BATCH, :], in_=sin[0, 0])
-        x_sb = keep.tile([P, FEATURES], BF16)
+        x_sb = keep.tile([P, FEATURES], BF16, align_bytes=256)
         nc.sync.dma_start(out=x_sb[0:P:BATCH, :], in_=x[0])
         nc.scalar.dma_start(out=x_sb[1:P:BATCH, :], in_=x[1])
         nc.scalar.dma_start(out=gain_rows[0:1, 0:HEAD], in_=q_norm_w.unsqueeze(0))
@@ -82,7 +82,7 @@ def tile_qwen3attention_pa_k_kernel(
             words, n_cols = weights[plan[n][0]]
             first_g = plan[n][1]
             groups_per_load = LOAD_WORDS // n_cols
-            w_sb = stream.tile([P, LOAD_WORDS], I32, align_bytes=64, tag="w", name="w_%d" % n)
+            w_sb = stream.tile([P, LOAD_WORDS], I32, align_bytes=256, tag="w", name="w_%d" % n)
             source = words[first_g : first_g + groups_per_load].rearrange("g p n j -> p g (n j)")
             if n % 2 == 1 and n != len(plan) - 1:
                 nc.scalar.dma_start(
@@ -99,7 +99,7 @@ def tile_qwen3attention_pa_k_kernel(
             issue(n)
 
         def load_scale_planes(scales, n_cols, label):
-            planes = keep.tile([P, (GROUPS // SHARED) * n_cols], U8, align_bytes=64, name="planes_" + label)
+            planes = keep.tile([P, (GROUPS // SHARED) * n_cols], U8, align_bytes=256, name="planes_" + label)
             nc.vector.memset(planes[:].bitcast(I32), 0)
             for c in range(GROUPS // SHARED):
                 for quadrant in range(QUADRANTS):
@@ -210,7 +210,7 @@ def tile_qwen3attention_pa_k_kernel(
             squares = work.tile([P, heads * HEAD], F32, tag="squares")
             straight_part = work.tile([P, heads * HEAD], F32, tag="straight_part")
             crossed_part = work.tile([P, heads * HEAD], F32, tag="crossed_part")
-            result = work.tile([P, heads * HEAD], F32, tag="result", bufs=RESULTS)
+            result = work.tile([P, heads * HEAD], F32, tag="result", bufs=RESULTS, align_bytes=256)
             sum_sq = work.tile([P, heads], F32, tag="sum_sq")
             mean_sq = work.tile([P, heads], F32, tag="mean_sq")
             rms = work.tile([P, heads], F32, tag="rms")
@@ -278,7 +278,7 @@ def tile_qwen3attention_pa_k_kernel(
             multiply(n, v_planes, v_banks)
         store(q_result, out_0)
         store(k_result, out_1)
-        v_result = work.tile([P, V_COLS], F32, tag="result", bufs=RESULTS)
+        v_result = work.tile([P, V_COLS], F32, tag="result", bufs=RESULTS, align_bytes=256)
         nc.vector.tensor_copy(out=v_result[:, 0:BANK], in_=v_banks[0][:])
         nc.scalar.copy(out=v_result[:, BANK : 2 * BANK], in_=v_banks[1][:])
         store(v_result, out_2)

@@ -37,7 +37,8 @@ WORDS_PER_GROUP = K_PASS // 2
 
 LOAD_WORDS = 2048
 W_BUFS = 12
-RESULTS = 3
+BANKS = 8
+POSITIONS = 64
 
 FLOPS = 2 * P * FEATURES * (Q_COLS + K_COLS + V_COLS)
 
@@ -52,7 +53,10 @@ def tile_qwen3attention_pa_k_kernel(
         keep = ctx.enter_context(tc.tile_pool(name="keep", bufs=1))
         stream = ctx.enter_context(tc.tile_pool(name="stream", bufs=W_BUFS))
         work = ctx.enter_context(tc.tile_pool(name="work", bufs=1))
-        psum = ctx.enter_context(tc.psum_pool(name="psum", bufs=8))
+        psum = ctx.enter_context(tc.psum_pool(name="psum", bufs=1))
+
+        def bank_tile(index, label):
+            return psum.tile([P, BANK], F32, tag="bank%d" % (index % BANKS), name="%s_%d" % (label, index))
 
         identity = keep.tile([P, P], F32)
         make_identity(nc, identity[:])
@@ -84,7 +88,14 @@ def tile_qwen3attention_pa_k_kernel(
             groups_per_load = LOAD_WORDS // n_cols
             w_sb = stream.tile([P, LOAD_WORDS], I32, align_bytes=256, tag="w", name="w_%d" % n)
             source = words[first_g : first_g + groups_per_load].rearrange("g p n j -> p g (n j)")
-            if n % 2 == 1 and n != len(plan) - 1:
+            if n == len(plan) - 1:
+                nc.sync.dma_start(out=w_sb[:, 0:n_cols], in_=source[:, 0, :].bitcast(I32))
+                for j in range(n_cols // BANK):
+                    nc.sync.dma_start(
+                        out=w_sb[:, n_cols + j * BANK : n_cols + (j + 1) * BANK],
+                        in_=source[:, 1, j * BANK * PACK : (j + 1) * BANK * PACK].bitcast(I32),
+                    )
+            elif n % 2 == 1:
                 nc.scalar.dma_start(
                     out=w_sb[:].bitcast(F32).rearrange("p (g n) -> p g n", g=groups_per_load),
                     in_=source.bitcast(F32),
@@ -126,7 +137,7 @@ def tile_qwen3attention_pa_k_kernel(
         for piece in range(X_PIECES):
             for half_piece in range(banks_per_piece):
                 bank = piece * banks_per_piece + half_piece
-                flipped = psum.tile([P, BANK], F32, tag="bank")
+                flipped = bank_tile(bank, "flipped")
                 for i in range(groups_per_bank):
                     g = bank * groups_per_bank + i
                     for u in range(2):
@@ -149,7 +160,7 @@ def tile_qwen3attention_pa_k_kernel(
                 in_=x_grouped[:, piece * GROUPS_PER_PIECE * K_PASS : (piece + 1) * GROUPS_PER_PIECE * K_PASS],
             )
 
-        gains = psum.tile([P, BANK], F32, tag="bank")
+        gains = bank_tile(0, "gains")
         nc.tensor.matmul(out=gains[:, 0 : 2 * HEAD], lhsT=ones[:], rhs=gain_rows[:], start=True, stop=True)
         gains_by_half = gains[:, 0 : 2 * HEAD].rearrange("p (w h d) -> p w h d", w=2, h=2)
         neg_sin = keep.tile([P, HALF], F32)
@@ -171,10 +182,8 @@ def tile_qwen3attention_pa_k_kernel(
             in1=sin_sb[:].unsqueeze(1).to_broadcast([P, 2, HALF]), op=MULT,
         )
 
-        def open_banks(n_cols, label):
-            return [
-                psum.tile([P, BANK], F32, tag="bank", name="acc_%s_%d" % (label, j)) for j in range(n_cols // BANK)
-            ]
+        def open_banks(first_bank, n_cols, label):
+            return [bank_tile(first_bank + j, "acc_" + label) for j in range(n_cols // BANK)]
 
         def multiply(n, planes, banks):
             n_cols = weights[plan[n][0]][1]
@@ -210,7 +219,7 @@ def tile_qwen3attention_pa_k_kernel(
             squares = work.tile([P, heads * HEAD], F32, tag="squares")
             straight_part = work.tile([P, heads * HEAD], F32, tag="straight_part")
             crossed_part = work.tile([P, heads * HEAD], F32, tag="crossed_part")
-            result = work.tile([P, heads * HEAD], F32, tag="result", bufs=RESULTS, align_bytes=256)
+            result = work.tile([P, heads * HEAD], F32, tag="result_%d" % weight, align_bytes=256)
             sum_sq = work.tile([P, heads], F32, tag="sum_sq")
             mean_sq = work.tile([P, heads], F32, tag="mean_sq")
             rms = work.tile([P, heads], F32, tag="rms")
@@ -259,26 +268,72 @@ def tile_qwen3attention_pa_k_kernel(
 
             return finish
 
+        q_heads = Q_COLS // HEAD
+        run = BATCH * POSITIONS * q_heads // P
+        runs = POSITIONS // run
+
+        def turn(result):
+            turned = work.tile([P, run * P], F32, tag="turned")
+            by_l = turned[:].rearrange("p (l b c) -> p l b c", l=run, b=BATCH)
+            per_bank = HEADS_PER_BANK * runs
+            for j in range(q_heads // HEADS_PER_BANK):
+                flipped = bank_tile(j, "turn")
+                for i in range(HEADS_PER_BANK):
+                    h = j * HEADS_PER_BANK + i
+                    nc.tensor.transpose(
+                        out=flipped[:, i * P : (i + 1) * P], in_=result[:, h * HEAD : (h + 1) * HEAD],
+                        identity=identity[:],
+                    )
+                copy_out = nc.vector.tensor_copy if j % 2 == 0 else nc.scalar.copy
+                copy_out(
+                    out=by_l[:, :, :, j * per_bank : (j + 1) * per_bank],
+                    in_=flipped[:].rearrange("p (c l b) -> p l b c", l=run, b=BATCH),
+                )
+            return turned
+
+        def turn_back(turned):
+            rows = work.tile([P, run * HEAD], F32, tag="rows", align_bytes=256)
+            for j in range(run * HEAD // BANK):
+                flipped = bank_tile(j, "back")
+                for i in range(BANK // HEAD):
+                    l = j * (BANK // HEAD) + i
+                    nc.tensor.transpose(
+                        out=flipped[:, i * HEAD : (i + 1) * HEAD], in_=turned[:, l * P : (l + 1) * P],
+                        identity=identity[:],
+                    )
+                copy_out = nc.vector.tensor_copy if j % 2 == 0 else nc.scalar.copy
+                copy_out(out=rows[:, j * BANK : (j + 1) * BANK], in_=flipped[:])
+            return rows
+
         q_loads = GROUPS * Q_COLS // LOAD_WORDS
         k_loads = GROUPS * K_COLS // LOAD_WORDS
         all_issued = len(plan) - W_BUFS
-        q_banks = open_banks(Q_COLS, "q")
+        q_banks = open_banks(0, Q_COLS, "q")
+        k_banks = open_banks(4, K_COLS, "k")
+        v_banks = open_banks(6, V_COLS, "v")
         for n in range(q_loads):
             multiply(n, q_planes, q_banks)
         finish_q = norm_and_rotate(q_banks, 0)
-        k_banks = open_banks(K_COLS, "k")
         for n in range(q_loads, all_issued):
             multiply(n, k_planes, k_banks)
         q_result = finish_q()
         for n in range(all_issued, q_loads + k_loads):
             multiply(n, k_planes, k_banks)
+        q_turned = turn(q_result)
         k_result = norm_and_rotate(k_banks, 1)()
-        v_banks = open_banks(V_COLS, "v")
-        for n in range(q_loads + k_loads, len(plan)):
+        v_first = q_loads + k_loads
+        for n in range(v_first, v_first + 2):
             multiply(n, v_planes, v_banks)
-        store(q_result, out_0)
+        q_rows = turn_back(q_turned)
+        for n in range(v_first + 2, len(plan)):
+            multiply(n, v_planes, v_banks)
+        nc.sync.dma_start(out=out_0.rearrange("b h (g l) d -> (b h g) (l d)", l=run), in_=q_rows[:])
         store(k_result, out_1)
-        v_result = work.tile([P, V_COLS], F32, tag="result", bufs=RESULTS, align_bytes=256)
-        nc.vector.tensor_copy(out=v_result[:, 0:BANK], in_=v_banks[0][:])
-        nc.scalar.copy(out=v_result[:, BANK : 2 * BANK], in_=v_banks[1][:])
-        store(v_result, out_2)
+        v_result = work.tile([P, V_COLS], F32, tag="result_v", align_bytes=256)
+        for j, copy_out in enumerate((nc.vector.tensor_copy, nc.scalar.copy)):
+            copy_out(out=v_result[:, j * BANK : (j + 1) * BANK], in_=v_banks[j][:])
+            for b in range(BATCH):
+                nc.scalar.dma_start(
+                    out=out_2[b, j * HEADS_PER_BANK : (j + 1) * HEADS_PER_BANK].rearrange("h t d -> t h d"),
+                    in_=v_result[b:P:BATCH, j * BANK : (j + 1) * BANK].rearrange("p (h d) -> p h d", d=HEAD),
+                )

from contextlib import ExitStack

import concourse.mybir as mybir
from concourse.masks import make_identity

F32 = mybir.dt.float32
BF16 = mybir.dt.bfloat16
U8 = mybir.dt.uint8
I32 = mybir.dt.int32
U32 = mybir.dt.uint32
FP8X4 = mybir.dt.float8_e4m3fn_x4
MULT = mybir.AluOpType.mult
ADD = mybir.AluOpType.add

P = 128
PACK = 4
K_PASS = P * PACK
BATCH = 2
FEATURES = 8192
GROUPS = FEATURES // K_PASS
HEAD = 128
HALF = HEAD // 2
Q_COLS = 2048
K_COLS = 1024
V_COLS = 1024
BANK = 512
HEADS_PER_BANK = BANK // HEAD
EPS = 1e-6

SHARED = 4
LIVE_ROWS = 4
QUADRANTS = 4

X_PIECES = 4
GROUPS_PER_PIECE = GROUPS // X_PIECES
WORDS_PER_GROUP = K_PASS // 2

LOAD_WORDS = 2048
W_BUFS = 12
BANKS = 8
POSITIONS = 64

FLOPS = 2 * P * FEATURES * (Q_COLS + K_COLS + V_COLS)


def tile_qwen3attention_pa_k_kernel(
    tc, x, cos, sin, wq_words, wq_scales, wk_words, wk_scales, wv_words, wv_scales,
    q_norm_w, k_norm_w, out_0, out_1, out_2,
):
    nc = tc.nc
    with ExitStack() as ctx:
        ctx.enter_context(tc.manual_schedule())
        keep = ctx.enter_context(tc.tile_pool(name="keep", bufs=1))
        stream = ctx.enter_context(tc.tile_pool(name="stream", bufs=W_BUFS))
        work = ctx.enter_context(tc.tile_pool(name="work", bufs=1))
        psum = ctx.enter_context(tc.psum_pool(name="psum", bufs=1))

        def bank_tile(index, label):
            return psum.tile([P, BANK], F32, tag="bank%d" % (index % BANKS), name="%s_%d" % (label, index))

        identity = keep.tile([P, P], F32)
        make_identity(nc, identity[:])
        cos_sb = keep.tile([P, HALF], BF16)
        sin_sb = keep.tile([P, HALF], BF16)
        gain_rows = keep.tile([P, 2 * HEAD], BF16)
        ones = keep.tile([P, P], BF16)
        nc.vector.memset(gain_rows[:], 0.0)
        nc.vector.memset(ones[:], 1.0)
        for b in range(BATCH):
            nc.scalar.dma_start(out=cos_sb[b:P:BATCH, :], in_=cos[0, 0])
            nc.scalar.dma_start(out=sin_sb[b:P:BATCH, :], in_=sin[0, 0])
        x_sb = keep.tile([P, FEATURES], BF16, align_bytes=256)
        nc.sync.dma_start(out=x_sb[0:P:BATCH, :], in_=x[0])
        nc.scalar.dma_start(out=x_sb[1:P:BATCH, :], in_=x[1])
        nc.scalar.dma_start(out=gain_rows[0:1, 0:HEAD], in_=q_norm_w.unsqueeze(0))
        nc.scalar.dma_start(out=gain_rows[0:1, HEAD : 2 * HEAD], in_=k_norm_w.unsqueeze(0))

        weights = ((wq_words, Q_COLS), (wk_words, K_COLS), (wv_words, V_COLS))
        plan = []
        for w_index in range(len(weights)):
            for first_g in range(0, GROUPS, LOAD_WORDS // weights[w_index][1]):
                plan.append((w_index, first_g))
        loaded = []

        def issue(n):
            words, n_cols = weights[plan[n][0]]
            first_g = plan[n][1]
            groups_per_load = LOAD_WORDS // n_cols
            w_sb = stream.tile([P, LOAD_WORDS], I32, align_bytes=256, tag="w", name="w_%d" % n)
            source = words[first_g : first_g + groups_per_load].rearrange("g p n j -> p g (n j)")
            if n == len(plan) - 1:
                nc.sync.dma_start(out=w_sb[:, 0:n_cols], in_=source[:, 0, :].bitcast(I32))
                for j in range(n_cols // BANK):
                    nc.sync.dma_start(
                        out=w_sb[:, n_cols + j * BANK : n_cols + (j + 1) * BANK],
                        in_=source[:, 1, j * BANK * PACK : (j + 1) * BANK * PACK].bitcast(I32),
                    )
            elif n % 2 == 1:
                nc.scalar.dma_start(
                    out=w_sb[:].bitcast(F32).rearrange("p (g n) -> p g n", g=groups_per_load),
                    in_=source.bitcast(F32),
                )
            else:
                nc.sync.dma_start(
                    out=w_sb[:].rearrange("p (g n) -> p g n", g=groups_per_load), in_=source.bitcast(I32)
                )
            loaded.append(w_sb)

        for n in range(W_BUFS):
            issue(n)

        def load_scale_planes(scales, n_cols, label):
            planes = keep.tile([P, (GROUPS // SHARED) * n_cols], U8, align_bytes=256, name="planes_" + label)
            nc.vector.memset(planes[:].bitcast(I32), 0)
            for c in range(GROUPS // SHARED):
                for quadrant in range(QUADRANTS):
                    first_row = 32 * quadrant
                    nc.gpsimd.dma_start(
                        out=planes[first_row : first_row + SHARED * LIVE_ROWS, c * n_cols : (c + 1) * n_cols].bitcast(F32),
                        in_=scales[
                            SHARED * c : SHARED * (c + 1), LIVE_ROWS * quadrant : LIVE_ROWS * (quadrant + 1), :
                        ].bitcast(F32),
                    )
            return planes

        q_planes = load_scale_planes(wq_scales, Q_COLS, "q")
        k_planes = load_scale_planes(wk_scales, K_COLS, "k")
        v_planes = load_scale_planes(wv_scales, V_COLS, "v")

        x_words = x_sb[:].bitcast(F32)
        x_grouped = keep.tile([P, GROUPS * P * PACK], BF16, align_bytes=64)
        grouped_words = x_grouped[:].bitcast(F32)
        x_codes = keep.tile([P, GROUPS * P], U32, align_bytes=64)
        x_plane = keep.tile([P, GROUPS * P], U8, align_bytes=64)
        groups_per_bank = BANK // (2 * P)
        banks_per_piece = GROUPS_PER_PIECE // groups_per_bank
        for piece in range(X_PIECES):
            for half_piece in range(banks_per_piece):
                bank = piece * banks_per_piece + half_piece
                flipped = bank_tile(bank, "flipped")
                for i in range(groups_per_bank):
                    g = bank * groups_per_bank + i
                    for u in range(2):
                        nc.tensor.transpose(
                            out=flipped[:, (2 * i + u) * P : (2 * i + u + 1) * P],
                            in_=x_words[:, WORDS_PER_GROUP * g + u : WORDS_PER_GROUP * (g + 1) : 2],
                            identity=identity[:],
                        )
                copy_out = nc.vector.tensor_copy if bank % 2 == 0 else nc.scalar.copy
                copy_out(
                    out=grouped_words[:, bank * BANK : (bank + 1) * BANK].rearrange(
                        "p (g r u) -> p g r u", g=groups_per_bank, u=2
                    ),
                    in_=flipped[:].rearrange("p (g u r) -> p g r u", g=groups_per_bank, u=2),
                )
            tokens = slice(piece * GROUPS_PER_PIECE * P, (piece + 1) * GROUPS_PER_PIECE * P)
            nc.vector.quantize_mx(
                out=x_codes[:, tokens].bitcast(FP8X4),
                scales=x_plane[:, tokens],
                in_=x_grouped[:, piece * GROUPS_PER_PIECE * K_PASS : (piece + 1) * GROUPS_PER_PIECE * K_PASS],
            )

        gains = bank_tile(0, "gains")
        nc.tensor.matmul(out=gains[:, 0 : 2 * HEAD], lhsT=ones[:], rhs=gain_rows[:], start=True, stop=True)
        gains_by_half = gains[:, 0 : 2 * HEAD].rearrange("p (w h d) -> p w h d", w=2, h=2)
        neg_sin = keep.tile([P, HALF], F32)
        nc.vector.tensor_scalar_mul(out=neg_sin[:], in0=sin_sb[:], scalar1=-1.0)
        straight = keep.tile([P, 2, 2, HALF], F32)
        crossed = keep.tile([P, 2, 2, HALF], F32)
        nc.vector.tensor_tensor(
            out=straight[:].rearrange("p w h d -> p (w h) d"),
            in0=gains[:, 0 : 2 * HEAD].rearrange("p (a d) -> p a d", d=HALF),
            in1=cos_sb[:].unsqueeze(1).to_broadcast([P, 4, HALF]),
            op=MULT,
        )
        nc.vector.tensor_tensor(
            out=crossed[:, :, 0, :], in0=gains_by_half[:, :, 1, :],
            in1=neg_sin[:].unsqueeze(1).to_broadcast([P, 2, HALF]), op=MULT,
        )
        nc.vector.tensor_tensor(
            out=crossed[:, :, 1, :], in0=gains_by_half[:, :, 0, :],
            in1=sin_sb[:].unsqueeze(1).to_broadcast([P, 2, HALF]), op=MULT,
        )

        def open_banks(first_bank, n_cols, label):
            return [bank_tile(first_bank + j, "acc_" + label) for j in range(n_cols // BANK)]

        def multiply(n, planes, banks):
            n_cols = weights[plan[n][0]][1]
            first_g = plan[n][1]
            w_sb = loaded[n]
            for i in range(LOAD_WORDS // n_cols):
                g = first_g + i
                first = LIVE_ROWS * (g % SHARED)
                for j, acc in enumerate(banks):
                    nc.tensor.matmul_mx(
                        out=acc[:],
                        lhsT=x_codes[:, g * P : (g + 1) * P].bitcast(FP8X4),
                        lhsT_scale=x_plane[:, g * P : (g + 1) * P],
                        rhs=w_sb[:, i * n_cols + j * BANK : i * n_cols + (j + 1) * BANK].bitcast(FP8X4),
                        rhs_scale=planes[
                            first:P, (g // SHARED) * n_cols + j * BANK : (g // SHARED) * n_cols + (j + 1) * BANK
                        ],
                        start=(g == 0),
                        stop=(g == GROUPS - 1),
                    )
            if n + W_BUFS < len(plan):
                issue(n + W_BUFS)

        def store(result, out):
            for b in range(BATCH):
                nc.sync.dma_start(
                    out=out[b].rearrange("h t d -> t h d"),
                    in_=result[b:P:BATCH, :].rearrange("p (h d) -> p h d", d=HEAD),
                )

        def norm_and_rotate(banks, weight):
            heads = len(banks) * HEADS_PER_BANK
            squares = work.tile([P, heads * HEAD], F32, tag="squares")
            straight_part = work.tile([P, heads * HEAD], F32, tag="straight_part")
            crossed_part = work.tile([P, heads * HEAD], F32, tag="crossed_part")
            result = work.tile([P, heads * HEAD], F32, tag="result_%d" % weight, align_bytes=256)
            sum_sq = work.tile([P, heads], F32, tag="sum_sq")
            mean_sq = work.tile([P, heads], F32, tag="mean_sq")
            rms = work.tile([P, heads], F32, tag="rms")
            inv_rms = work.tile([P, heads], F32, tag="inv_rms")
            for j, acc in enumerate(banks):
                cols = slice(j * BANK, (j + 1) * BANK)
                nc.scalar.square(out=squares[:, cols], in_=acc[:])
                nc.vector.tensor_reduce(
                    out=sum_sq[:, j * HEADS_PER_BANK : (j + 1) * HEADS_PER_BANK],
                    in_=squares[:, cols].rearrange("p (h d) -> p h d", d=HEAD),
                    axis=mybir.AxisListType.X,
                    op=ADD,
                )
                nc.vector.tensor_tensor(
                    out=straight_part[:, cols].rearrange("p (h d) -> p h d", d=HEAD),
                    in0=acc[:].rearrange("p (h d) -> p h d", d=HEAD),
                    in1=straight[:, weight].rearrange("p h d -> p (h d)").unsqueeze(1).to_broadcast(
                        [P, HEADS_PER_BANK, HEAD]
                    ),
                    op=MULT,
                )
                acc_halves = acc[:].rearrange("p (h s d) -> p h s d", s=2, d=HALF)
                crossed_halves = crossed_part[:, cols].rearrange("p (h s d) -> p h s d", s=2, d=HALF)
                for s in range(2):
                    nc.vector.tensor_tensor(
                        out=crossed_halves[:, :, s, :],
                        in0=acc_halves[:, :, 1 - s, :],
                        in1=crossed[:, weight, s, :].unsqueeze(1).to_broadcast([P, HEADS_PER_BANK, HALF]),
                        op=MULT,
                    )

            def finish():
                nc.vector.tensor_scalar(
                    out=mean_sq[:], in0=sum_sq[:], scalar1=1.0 / HEAD, scalar2=EPS, op0=MULT, op1=ADD
                )
                nc.scalar.sqrt(out=rms[:], in_=mean_sq[:])
                nc.vector.reciprocal(out=inv_rms[:], in_=rms[:])
                nc.vector.tensor_tensor(out=straight_part[:], in0=straight_part[:], in1=crossed_part[:], op=ADD)
                nc.vector.tensor_tensor(
                    out=result[:].rearrange("p (h d) -> p h d", d=HEAD),
                    in0=straight_part[:].rearrange("p (h d) -> p h d", d=HEAD),
                    in1=inv_rms[:].unsqueeze(2).to_broadcast([P, heads, HEAD]),
                    op=MULT,
                )
                return result

            return finish

        q_heads = Q_COLS // HEAD
        run = BATCH * POSITIONS * q_heads // P
        runs = POSITIONS // run

        def turn(result):
            turned = work.tile([P, run * P], F32, tag="turned")
            by_l = turned[:].rearrange("p (l b c) -> p l b c", l=run, b=BATCH)
            per_bank = HEADS_PER_BANK * runs
            for j in range(q_heads // HEADS_PER_BANK):
                flipped = bank_tile(j, "turn")
                for i in range(HEADS_PER_BANK):
                    h = j * HEADS_PER_BANK + i
                    nc.tensor.transpose(
                        out=flipped[:, i * P : (i + 1) * P], in_=result[:, h * HEAD : (h + 1) * HEAD],
                        identity=identity[:],
                    )
                copy_out = nc.vector.tensor_copy if j % 2 == 0 else nc.scalar.copy
                copy_out(
                    out=by_l[:, :, :, j * per_bank : (j + 1) * per_bank],
                    in_=flipped[:].rearrange("p (c l b) -> p l b c", l=run, b=BATCH),
                )
            return turned

        def turn_back(turned):
            rows = work.tile([P, run * HEAD], F32, tag="rows", align_bytes=256)
            for j in range(run * HEAD // BANK):
                flipped = bank_tile(j, "back")
                for i in range(BANK // HEAD):
                    l = j * (BANK // HEAD) + i
                    nc.tensor.transpose(
                        out=flipped[:, i * HEAD : (i + 1) * HEAD], in_=turned[:, l * P : (l + 1) * P],
                        identity=identity[:],
                    )
                copy_out = nc.vector.tensor_copy if j % 2 == 0 else nc.scalar.copy
                copy_out(out=rows[:, j * BANK : (j + 1) * BANK], in_=flipped[:])
            return rows

        q_loads = GROUPS * Q_COLS // LOAD_WORDS
        k_loads = GROUPS * K_COLS // LOAD_WORDS
        all_issued = len(plan) - W_BUFS
        q_banks = open_banks(0, Q_COLS, "q")
        k_banks = open_banks(4, K_COLS, "k")
        v_banks = open_banks(6, V_COLS, "v")
        for n in range(q_loads):
            multiply(n, q_planes, q_banks)
        finish_q = norm_and_rotate(q_banks, 0)
        for n in range(q_loads, all_issued):
            multiply(n, k_planes, k_banks)
        q_result = finish_q()
        for n in range(all_issued, q_loads + k_loads):
            multiply(n, k_planes, k_banks)
        q_turned = turn(q_result)
        k_result = norm_and_rotate(k_banks, 1)()
        v_first = q_loads + k_loads
        for n in range(v_first, v_first + 2):
            multiply(n, v_planes, v_banks)
        q_rows = turn_back(q_turned)
        for n in range(v_first + 2, len(plan)):
            multiply(n, v_planes, v_banks)
        nc.sync.dma_start(out=out_0.rearrange("b h (g l) d -> (b h g) (l d)", l=run), in_=q_rows[:])
        store(k_result, out_1)
        v_result = work.tile([P, V_COLS], F32, tag="result_v", align_bytes=256)
        for j, copy_out in enumerate((nc.vector.tensor_copy, nc.scalar.copy)):
            copy_out(out=v_result[:, j * BANK : (j + 1) * BANK], in_=v_banks[j][:])
            for b in range(BATCH):
                nc.scalar.dma_start(
                    out=out_2[b, j * HEADS_PER_BANK : (j + 1) * HEADS_PER_BANK].rearrange("h t d -> t h d"),
                    in_=v_result[b:P:BATCH, j * BANK : (j + 1) * BANK].rearrange("p (h d) -> p h d", d=HEAD),
                )
